import numpy as np
import ml_dtypes


def mxq(x, axis, fmt="e4m3"):
    dtype, down = {"e4m3": (ml_dtypes.float8_e4m3fn, 7), "e5m2": (ml_dtypes.float8_e5m2, 14)}[fmt]
    v = np.moveaxis(np.asarray(x, np.float32).astype(ml_dtypes.bfloat16).astype(np.float64), axis, -1)
    blocks = v.reshape(v.shape[:-1] + (-1, 32))
    amax = np.abs(blocks).max(-1, keepdims=True)
    byte = np.maximum(np.where(amax > 0, np.frexp(amax)[1] - 1 + 127, 0) - down, 1)
    scale = np.exp2(byte - 127.0)
    codes = (blocks / scale).astype(np.float32).astype(dtype).astype(np.float64)
    return np.moveaxis((codes * scale).reshape(v.shape), -1, axis)


WIDE = False


def mx_kscale(k):
    if not WIDE:
        return np.ones(k)
    levels = np.array([10, -10, 5, -5, 0])
    a = np.random.permutation(np.resize(levels, k // 512 * 4)).reshape(k // 512, 4)
    idx = np.arange(k)
    return np.exp2(a[idx // 512, idx % 128 // 32])


BF16 = ml_dtypes.bfloat16


def bf(x):
    return np.asarray(x, np.float32).astype(BF16)


def f64(x):
    return np.asarray(x).astype(np.float64)


B, HALF, MID = 128, 128, 1024
D = 2 * HALF


def setup_inputs():
    s, t = mx_kscale(MID), mx_kscale(MID)
    return {"x": bf(np.random.standard_normal((B, D))),
            "h3": bf(np.maximum(np.random.standard_normal((B, MID)), 0.0) * s),
            "W4": bf(np.random.standard_normal((MID, MID)) * np.sqrt(2.0 / MID) / s[:, None] * t),
            "b4": bf(np.random.standard_normal(MID) * 0.2 * t),
            "W5": bf(np.random.standard_normal((MID, HALF)) * np.sqrt(2.0 / MID) / t[:, None]),
            "b5": bf(np.random.standard_normal(HALF) * 0.2)}


def reference(x, h3, W4, b4, W5, b5):
    x = f64(x)
    even = x[:, 0::2]
    odd = x[:, 1::2]
    h4 = np.maximum((mxq(f64(h3), 1, "e4m3") @ mxq(f64(W4), 0, "e4m3")) + f64(b4), 0.0)
    m = (mxq(h4, 1, "e4m3") @ mxq(f64(W5), 0, "e4m3")) + f64(b5)
    transformed = even + m
    return np.stack([transformed, odd], axis=2).reshape(B, -1)

@@ -1,0 +1,153 @@
+from contextlib import ExitStack
+
+import concourse.mybir as mybir
+from concourse.masks import make_identity
+
+BF16 = mybir.dt.bfloat16
+F32 = mybir.dt.float32
+U32 = mybir.dt.uint32
+U8 = mybir.dt.uint8
+FP8X4 = mybir.dt.float8_e4m3fn_x4
+ADD = mybir.AluOpType.add
+
+P = 128
+PACK = 4
+K_PASS = P * PACK
+BATCH = 128
+MID = 1024
+HALF = 128
+PASSES = MID // K_PASS
+
+SCALAR_GROUPS = 88
+
+FLOPS = 2 * BATCH * MID * MID + 2 * BATCH * MID * HALF
+
+
+def tile_additivecoupling_pa_s_kernel(tc, x, h3, W4, b4, W5, b5, out):
+    nc = tc.nc
+    with ExitStack() as stack:
+        sbuf = stack.enter_context(tc.tile_pool(name="sbuf", bufs=1))
+        psum = stack.enter_context(tc.psum_pool(name="psum", bufs=1))
+
+        ident = sbuf.tile([P, P], F32)
+        make_identity(nc, ident[:])
+        ones = sbuf.tile([P, BATCH], BF16)
+        nc.vector.memset(ones[:], 1.0)
+        b5_rows = sbuf.tile([P, HALF], BF16)
+        nc.vector.memset(b5_rows[:], 0.0)
+
+        w4_raw = sbuf.tile([P, PASSES, PACK, MID], BF16)
+        w4_rows = W4.rearrange("(g p j) n -> p g j n", g=PASSES, j=PACK)
+        h3_sb = sbuf.tile([BATCH, MID], BF16)
+        w5_raw = sbuf.tile([P, PASSES, PACK, HALF], BF16)
+        x_sb = sbuf.tile([BATCH, 2 * HALF], BF16)
+        b4_sb = sbuf.tile([P, PASSES, PACK], BF16)
+
+        def load_w4(g, half):
+            cols = slice(half * K_PASS, (half + 1) * K_PASS)
+            nc.sync.dma_start(out=w4_raw[:, g, :, cols], in_=w4_rows[:, g, :, cols])
+
+        nc.scalar.dma_start(out=x_sb[:], in_=x)
+        nc.scalar.dma_start(out=b5_rows[0:1, :], in_=b5.rearrange("(o j) -> o j", o=1))
+        nc.scalar.dma_start(out=b4_sb[:], in_=b4.rearrange("(g c t) -> c g t", g=PASSES, t=PACK))
+        load_w4(0, 0)
+        nc.sync.dma_start(out=h3_sb[:], in_=h3)
+        load_w4(1, 0)
+        nc.sync.dma_start(out=w5_raw[:], in_=W5.rearrange("(g c t) j -> c g t j", g=PASSES, t=PACK))
+        load_w4(0, 1)
+        load_w4(1, 1)
+
+        res = sbuf.tile([BATCH, 2 * HALF], F32)
+        res_even = res[:].rearrange("b (j two) -> b j two", two=2)[:, :, 0]
+        nc.scalar.copy(out=res[:], in_=x_sb[:])
+        b5_all = psum.tile([BATCH, HALF], F32)
+        nc.tensor.matmul(b5_all[:], lhsT=ones[:], rhs=b5_rows[:], start=True, stop=True)
+        nc.vector.tensor_tensor(out=res_even, in0=b5_all[:], in1=res_even, op=ADD)
+
+        h3_words = h3_sb[:].bitcast(F32).rearrange("b (g p u) -> b g u p", g=PASSES, u=2)
+        h3_t = psum.tile([P, PASSES, 2, BATCH], F32)
+        for g in range(PASSES):
+            for u in range(2):
+                nc.tensor.transpose(h3_t[:, g, u, :], h3_words[:, g, u, :], ident[:])
+        h3_grouped = sbuf.tile([P, PASSES * BATCH * PACK], BF16, align_bytes=64)
+        nc.vector.tensor_copy(
+            out=h3_grouped[:].bitcast(F32).rearrange("p (g b u) -> p g b u", g=PASSES, u=2),
+            in_=h3_t[:].rearrange("p g u b -> p g b u"),
+        )
+        h3_codes = sbuf.tile([P, PASSES, BATCH], U32, align_bytes=64)
+        h3_scales = sbuf.tile([P, PASSES, BATCH], U8, align_bytes=64)
+        nc.vector.quantize_mx(
+            out=h3_codes[:].rearrange("p g b -> p (g b)").bitcast(FP8X4),
+            scales=h3_scales[:].rearrange("p g b -> p (g b)"),
+            in_=h3_grouped[:],
+        )
+
+        w5_grouped = sbuf.tile([P, PASSES, HALF, PACK], BF16, align_bytes=64)
+        nc.vector.tensor_copy(out=w5_grouped[:], in_=w5_raw[:].rearrange("c g t j -> c g j t"))
+        w5_codes = sbuf.tile([P, PASSES, HALF], U32, align_bytes=64)
+        w5_scales = sbuf.tile([P, PASSES, HALF], U8, align_bytes=64)
+        nc.vector.quantize_mx(
+            out=w5_codes[:].rearrange("c g j -> c (g j)").bitcast(FP8X4),
+            scales=w5_scales[:].rearrange("c g j -> c (g j)"),
+            in_=w5_grouped[:].rearrange("c g j t -> c (g j t)"),
+        )
+
+        w4_codes = sbuf.tile([P, PASSES, MID], U32, align_bytes=64)
+        w4_scales = sbuf.tile([P, PASSES, MID], U8, align_bytes=64)
+        h4_codes = sbuf.tile([P, PASSES, BATCH], U32, align_bytes=64)
+        h4_scales = sbuf.tile([P, PASSES, BATCH], U8, align_bytes=64)
+        m_acc = psum.tile([BATCH, HALF], F32)
+
+        for half in range(PASSES):
+            half_cols = slice(half * K_PASS, (half + 1) * K_PASS)
+            for g in range(PASSES):
+                w4_grouped = sbuf.tile([P, PACK, P, PACK], BF16, align_bytes=64, name="w4_grouped_%d%d" % (half, g))
+                dst = w4_grouped[:].rearrange("p t c j -> p c j t")
+                src = w4_raw[:, g, :, half_cols].rearrange("p j (c t) -> p c j t", t=PACK)
+                nc.scalar.copy(out=dst[:, :SCALAR_GROUPS], in_=src[:, :SCALAR_GROUPS])
+                nc.vector.tensor_copy(out=dst[:, SCALAR_GROUPS:], in_=src[:, SCALAR_GROUPS:])
+                nc.vector.quantize_mx(
+                    out=w4_codes[:, g, half_cols].bitcast(FP8X4),
+                    scales=w4_scales[:, g, half_cols],
+                    in_=w4_grouped[:].rearrange("p t c j -> p (t c j)"),
+                )
+
+            h4_acc = psum.tile([P, PACK, BATCH], F32, name="h4_acc_%d" % half)
+            for t in range(PACK):
+                cols = slice(half * K_PASS + t * P, half * K_PASS + (t + 1) * P)
+                for g in range(PASSES):
+                    nc.tensor.matmul_mx(
+                        out=h4_acc[:, t, :],
+                        lhsT=w4_codes[:, g, cols].bitcast(FP8X4),
+                        lhsT_scale=w4_scales[:, g, cols],
+                        rhs=h3_codes[:, g, :].bitcast(FP8X4),
+                        rhs_scale=h3_scales[:, g, :],
+                        start=(g == 0),
+                        stop=(g == PASSES - 1),
+                    )
+            h4_sum = sbuf.tile([P, BATCH, PACK], BF16, name="h4_sum_%d" % half)
+            nc.vector.tensor_tensor(
+                out=h4_sum[:],
+                in0=h4_acc[:].rearrange("c t b -> c b t"),
+                in1=b4_sb[:, half, :].unsqueeze(1).to_broadcast([P, BATCH, PACK]),
+                op=ADD,
+            )
+            h4_grouped = sbuf.tile([P, BATCH, PACK], BF16, align_bytes=64, name="h4_grouped_%d" % half)
+            nc.vector.tensor_scalar_max(out=h4_grouped[:], in0=h4_sum[:], scalar1=0.0)
+            nc.vector.quantize_mx(
+                out=h4_codes[:, half, :].bitcast(FP8X4),
+                scales=h4_scales[:, half, :],
+                in_=h4_grouped[:].rearrange("c b t -> c (b t)"),
+            )
+            nc.tensor.matmul_mx(
+                out=m_acc[:],
+                lhsT=h4_codes[:, half, :].bitcast(FP8X4),
+                lhsT_scale=h4_scales[:, half, :],
+                rhs=w5_codes[:, half, :].bitcast(FP8X4),
+                rhs_scale=w5_scales[:, half, :],
+                start=(half == 0),
+                stop=(half == PASSES - 1),
+            )
+
+        nc.vector.tensor_tensor(out=res_even, in0=m_acc[:], in1=res_even, op=ADD)
+        nc.sync.dma_start(out=out, in_=res[:])

@@ -18,7 +18,8 @@ MID = 1024
 HALF = 128
 PASSES = MID // K_PASS
 
-SCALAR_GROUPS = 88
+VECTOR_TILES = slice(0, 2)
+SCALAR_TILES = slice(2, 4)
 
 FLOPS = 2 * BATCH * MID * MID + 2 * BATCH * MID * HALF
 
@@ -28,6 +29,7 @@ def tile_additivecoupling_pa_s_kernel(tc, x, h3, W4, b4, W5, b5, out):
     with ExitStack() as stack:
         sbuf = stack.enter_context(tc.tile_pool(name="sbuf", bufs=1))
         psum = stack.enter_context(tc.psum_pool(name="psum", bufs=1))
+        stack.enter_context(tc.manual_schedule())
 
         ident = sbuf.tile([P, P], F32)
         make_identity(nc, ident[:])
@@ -36,104 +38,94 @@ def tile_additivecoupling_pa_s_kernel(tc, x, h3, W4, b4, W5, b5, out):
         b5_rows = sbuf.tile([P, HALF], BF16)
         nc.vector.memset(b5_rows[:], 0.0)
 
-        w4_raw = sbuf.tile([P, PASSES, PACK, MID], BF16)
+        w4_raw = {}
+        for half in range(PASSES):
+            for g in range(PASSES):
+                w4_raw[(half, g)] = sbuf.tile([P, PACK, K_PASS], BF16, name="w4_raw_%d%d" % (half, g))
         w4_rows = W4.rearrange("(g p j) n -> p g j n", g=PASSES, j=PACK)
         h3_sb = sbuf.tile([BATCH, MID], BF16)
         w5_raw = sbuf.tile([P, PASSES, PACK, HALF], BF16)
         x_sb = sbuf.tile([BATCH, 2 * HALF], BF16)
         b4_sb = sbuf.tile([P, PASSES, PACK], BF16)
 
-        def load_w4(g, half):
+        def load_w4(half, g):
             cols = slice(half * K_PASS, (half + 1) * K_PASS)
-            nc.sync.dma_start(out=w4_raw[:, g, :, cols], in_=w4_rows[:, g, :, cols])
+            nc.sync.dma_start(out=w4_raw[(half, g)][:], in_=w4_rows[:, g, :, cols])
 
         nc.scalar.dma_start(out=x_sb[:], in_=x)
         nc.scalar.dma_start(out=b5_rows[0:1, :], in_=b5.rearrange("(o j) -> o j", o=1))
         nc.scalar.dma_start(out=b4_sb[:], in_=b4.rearrange("(g c t) -> c g t", g=PASSES, t=PACK))
         load_w4(0, 0)
+        load_w4(0, 1)
         nc.sync.dma_start(out=h3_sb[:], in_=h3)
         load_w4(1, 0)
-        nc.sync.dma_start(out=w5_raw[:], in_=W5.rearrange("(g c t) j -> c g t j", g=PASSES, t=PACK))
-        load_w4(0, 1)
         load_w4(1, 1)
+        nc.sync.dma_start(out=w5_raw[:], in_=W5.rearrange("(g c t) j -> c g t j", g=PASSES, t=PACK))
 
-        res = sbuf.tile([BATCH, 2 * HALF], F32)
-        res_even = res[:].rearrange("b (j two) -> b j two", two=2)[:, :, 0]
-        nc.scalar.copy(out=res[:], in_=x_sb[:])
-        b5_all = psum.tile([BATCH, HALF], F32)
-        nc.tensor.matmul(b5_all[:], lhsT=ones[:], rhs=b5_rows[:], start=True, stop=True)
-        nc.vector.tensor_tensor(out=res_even, in0=b5_all[:], in1=res_even, op=ADD)
-
-        h3_words = h3_sb[:].bitcast(F32).rearrange("b (g p u) -> b g u p", g=PASSES, u=2)
-        h3_t = psum.tile([P, PASSES, 2, BATCH], F32)
-        for g in range(PASSES):
-            for u in range(2):
-                nc.tensor.transpose(h3_t[:, g, u, :], h3_words[:, g, u, :], ident[:])
-        h3_grouped = sbuf.tile([P, PASSES * BATCH * PACK], BF16, align_bytes=64)
-        nc.vector.tensor_copy(
-            out=h3_grouped[:].bitcast(F32).rearrange("p (g b u) -> p g b u", g=PASSES, u=2),
-            in_=h3_t[:].rearrange("p g u b -> p g b u"),
-        )
+        w4_grouped = {}
+        for half in range(PASSES):
+            for g in range(PASSES):
+                w4_grouped[(half, g)] = sbuf.tile(
+                    [P, PACK, P, PACK], BF16, align_bytes=64, name="w4_grouped_%d%d" % (half, g)
+                )
+        w4_codes = sbuf.tile([P, PASSES, PASSES, PACK, P], U32, align_bytes=64)
+        w4_scales = sbuf.tile([P, PASSES, PASSES, PACK, P], U8, align_bytes=64)
         h3_codes = sbuf.tile([P, PASSES, BATCH], U32, align_bytes=64)
         h3_scales = sbuf.tile([P, PASSES, BATCH], U8, align_bytes=64)
-        nc.vector.quantize_mx(
-            out=h3_codes[:].rearrange("p g b -> p (g b)").bitcast(FP8X4),
-            scales=h3_scales[:].rearrange("p g b -> p (g b)"),
-            in_=h3_grouped[:],
-        )
-
-        w5_grouped = sbuf.tile([P, PASSES, HALF, PACK], BF16, align_bytes=64)
-        nc.vector.tensor_copy(out=w5_grouped[:], in_=w5_raw[:].rearrange("c g t j -> c g j t"))
         w5_codes = sbuf.tile([P, PASSES, HALF], U32, align_bytes=64)
         w5_scales = sbuf.tile([P, PASSES, HALF], U8, align_bytes=64)
-        nc.vector.quantize_mx(
-            out=w5_codes[:].rearrange("c g j -> c (g j)").bitcast(FP8X4),
-            scales=w5_scales[:].rearrange("c g j -> c (g j)"),
-            in_=w5_grouped[:].rearrange("c g j t -> c (g j t)"),
-        )
-
-        w4_codes = sbuf.tile([P, PASSES, MID], U32, align_bytes=64)
-        w4_scales = sbuf.tile([P, PASSES, MID], U8, align_bytes=64)
         h4_codes = sbuf.tile([P, PASSES, BATCH], U32, align_bytes=64)
         h4_scales = sbuf.tile([P, PASSES, BATCH], U8, align_bytes=64)
+        h4_acc = {}
+        for half in range(PASSES):
+            h4_acc[half] = psum.tile([P, PACK, BATCH], F32, name="h4_acc_%d" % half)
         m_acc = psum.tile([BATCH, HALF], F32)
 
-        for half in range(PASSES):
-            half_cols = slice(half * K_PASS, (half + 1) * K_PASS)
-            for g in range(PASSES):
-                w4_grouped = sbuf.tile([P, PACK, P, PACK], BF16, align_bytes=64, name="w4_grouped_%d%d" % (half, g))
-                dst = w4_grouped[:].rearrange("p t c j -> p c j t")
-                src = w4_raw[:, g, :, half_cols].rearrange("p j (c t) -> p c j t", t=PACK)
-                nc.scalar.copy(out=dst[:, :SCALAR_GROUPS], in_=src[:, :SCALAR_GROUPS])
-                nc.vector.tensor_copy(out=dst[:, SCALAR_GROUPS:], in_=src[:, SCALAR_GROUPS:])
-                nc.vector.quantize_mx(
-                    out=w4_codes[:, g, half_cols].bitcast(FP8X4),
-                    scales=w4_scales[:, g, half_cols],
-                    in_=w4_grouped[:].rearrange("p t c j -> p (t c j)"),
-                )
+        def regroup_w4(half, g):
+            dst = w4_grouped[(half, g)][:]
+            src = w4_raw[(half, g)][:].rearrange("p j (c t) -> p t c j", t=PACK)
+            nc.vector.tensor_copy(
+                out=dst[:, VECTOR_TILES].rearrange("p t c j -> p c j t"),
+                in_=src[:, VECTOR_TILES].rearrange("p t c j -> p c j t"),
+            )
+            nc.scalar.copy(
+                out=dst[:, SCALAR_TILES].rearrange("p t c j -> p c j t"),
+                in_=src[:, SCALAR_TILES].rearrange("p t c j -> p c j t"),
+            )
 
-            h4_acc = psum.tile([P, PACK, BATCH], F32, name="h4_acc_%d" % half)
+        def quantise_w4(half, g, tiles):
+            nc.vector.quantize_mx(
+                out=w4_codes[:, g, half, tiles].rearrange("p t c -> p (t c)").bitcast(FP8X4),
+                scales=w4_scales[:, g, half, tiles].rearrange("p t c -> p (t c)"),
+                in_=w4_grouped[(half, g)][:, tiles].rearrange("p t c j -> p (t c j)"),
+            )
+
+        def first_layer(half):
             for t in range(PACK):
-                cols = slice(half * K_PASS + t * P, half * K_PASS + (t + 1) * P)
                 for g in range(PASSES):
                     nc.tensor.matmul_mx(
-                        out=h4_acc[:, t, :],
-                        lhsT=w4_codes[:, g, cols].bitcast(FP8X4),
-                        lhsT_scale=w4_scales[:, g, cols],
+                        out=h4_acc[half][:, t, :],
+                        lhsT=w4_codes[:, g, half, t, :].bitcast(FP8X4),
+                        lhsT_scale=w4_scales[:, g, half, t, :],
                         rhs=h3_codes[:, g, :].bitcast(FP8X4),
                         rhs_scale=h3_scales[:, g, :],
                         start=(g == 0),
                         stop=(g == PASSES - 1),
                     )
+
+        def bias_relu(half):
             h4_sum = sbuf.tile([P, BATCH, PACK], BF16, name="h4_sum_%d" % half)
             nc.vector.tensor_tensor(
                 out=h4_sum[:],
-                in0=h4_acc[:].rearrange("c t b -> c b t"),
+                in0=h4_acc[half][:].rearrange("c t b -> c b t"),
                 in1=b4_sb[:, half, :].unsqueeze(1).to_broadcast([P, BATCH, PACK]),
                 op=ADD,
             )
             h4_grouped = sbuf.tile([P, BATCH, PACK], BF16, align_bytes=64, name="h4_grouped_%d" % half)
             nc.vector.tensor_scalar_max(out=h4_grouped[:], in0=h4_sum[:], scalar1=0.0)
+            return h4_grouped
+
+        def second_layer(half, h4_grouped):
             nc.vector.quantize_mx(
                 out=h4_codes[:, half, :].bitcast(FP8X4),
                 scales=h4_scales[:, half, :],
@@ -148,6 +140,58 @@ def tile_additivecoupling_pa_s_kernel(tc, x, h3, W4, b4, W5, b5, out):
                 start=(half == 0),
                 stop=(half == PASSES - 1),
             )
+
+        res = sbuf.tile([BATCH, 2 * HALF], F32)
+        res_even = res[:].rearrange("b (j two) -> b j two", two=2)[:, :, 0]
+
+        regroup_w4(0, 0)
+        nc.scalar.copy(out=res[:], in_=x_sb[:])
+        quantise_w4(0, 0, VECTOR_TILES)
+
+        regroup_w4(0, 1)
+        h3_words = h3_sb[:].bitcast(F32).rearrange("b (g p u) -> b g u p", g=PASSES, u=2)
+        h3_t = psum.tile([P, PASSES, 2, BATCH], F32)
+        for g in range(PASSES):
+            for u in range(2):
+                nc.tensor.transpose(h3_t[:, g, u, :], h3_words[:, g, u, :], ident[:])
+        h3_grouped = sbuf.tile([P, PASSES * BATCH * PACK], BF16, align_bytes=64)
+        nc.scalar.copy(
+            out=h3_grouped[:].bitcast(F32).rearrange("p (g b u) -> p g b u", g=PASSES, u=2),
+            in_=h3_t[:].rearrange("p g u b -> p g b u"),
+        )
+        b5_all = psum.tile([BATCH, HALF], F32)
+        nc.tensor.matmul(b5_all[:], lhsT=ones[:], rhs=b5_rows[:], start=True, stop=True)
+        quantise_w4(0, 0, SCALAR_TILES)
+        quantise_w4(0, 1, VECTOR_TILES)
+        nc.vector.tensor_tensor(out=res_even, in0=b5_all[:], in1=res_even, op=ADD)
+        nc.vector.quantize_mx(
+            out=h3_codes[:].rearrange("p g b -> p (g b)").bitcast(FP8X4),
+            scales=h3_scales[:].rearrange("p g b -> p (g b)"),
+            in_=h3_grouped[:],
+        )
+
+        regroup_w4(1, 0)
+        quantise_w4(0, 1, SCALAR_TILES)
+        first_layer(0)
+        quantise_w4(1, 0, VECTOR_TILES)
+
+        regroup_w4(1, 1)
+        w5_grouped = sbuf.tile([P, PASSES, HALF, PACK], BF16, align_bytes=64)
+        nc.scalar.copy(out=w5_grouped[:], in_=w5_raw[:].rearrange("c g t j -> c g j t"))
+        quantise_w4(1, 0, SCALAR_TILES)
+        quantise_w4(1, 1, VECTOR_TILES)
+        quantise_w4(1, 1, SCALAR_TILES)
+        first_layer(1)
+
+        h4_grouped_0 = bias_relu(0)
+        nc.vector.quantize_mx(
+            out=w5_codes[:].rearrange("c g j -> c (g j)").bitcast(FP8X4),
+            scales=w5_scales[:].rearrange("c g j -> c (g j)"),
+            in_=w5_grouped[:].rearrange("c g j t -> c (g j t)"),
+        )
+        second_layer(0, h4_grouped_0)
+        h4_grouped_1 = bias_relu(1)
+        second_layer(1, h4_grouped_1)
 
         nc.vector.tensor_tensor(out=res_even, in0=m_acc[:], in1=res_even, op=ADD)
         nc.sync.dma_start(out=out, in_=res[:])

@@ -29,7 +29,6 @@ def tile_additivecoupling_pa_s_kernel(tc, x, h3, W4, b4, W5, b5, out):
     with ExitStack() as stack:
         sbuf = stack.enter_context(tc.tile_pool(name="sbuf", bufs=1))
         psum = stack.enter_context(tc.psum_pool(name="psum", bufs=1))
-        stack.enter_context(tc.manual_schedule())
 
         ident = sbuf.tile([P, P], F32)
         make_identity(nc, ident[:])

@@ -29,6 +29,7 @@ def tile_additivecoupling_pa_s_kernel(tc, x, h3, W4, b4, W5, b5, out):
     with ExitStack() as stack:
         sbuf = stack.enter_context(tc.tile_pool(name="sbuf", bufs=1))
         psum = stack.enter_context(tc.psum_pool(name="psum", bufs=1))
+        stack.enter_context(tc.manual_schedule())
 
         ident = sbuf.tile([P, P], F32)
         make_identity(nc, ident[:])
@@ -51,10 +52,10 @@ def tile_additivecoupling_pa_s_kernel(tc, x, h3, W4, b4, W5, b5, out):
             cols = slice(half * K_PASS, (half + 1) * K_PASS)
             nc.sync.dma_start(out=w4_raw[(half, g)][:], in_=w4_rows[:, g, :, cols])
 
-        nc.scalar.dma_start(out=x_sb[:], in_=x)
-        nc.scalar.dma_start(out=b5_rows[0:1, :], in_=b5.rearrange("(o j) -> o j", o=1))
-        nc.scalar.dma_start(out=b4_sb[:], in_=b4.rearrange("(g c t) -> c g t", g=PASSES, t=PACK))
         load_w4(0, 0)
+        nc.sync.dma_start(out=x_sb[:], in_=x)
+        nc.sync.dma_start(out=b5_rows[0:1, :], in_=b5.rearrange("(o j) -> o j", o=1))
+        nc.sync.dma_start(out=b4_sb[:], in_=b4.rearrange("(g c t) -> c g t", g=PASSES, t=PACK))
         load_w4(0, 1)
         nc.sync.dma_start(out=h3_sb[:], in_=h3)
         load_w4(1, 0)
@@ -113,23 +114,30 @@ def tile_additivecoupling_pa_s_kernel(tc, x, h3, W4, b4, W5, b5, out):
                     )
 
         def bias_relu(half):
-            h4_sum = sbuf.tile([P, BATCH, PACK], BF16, name="h4_sum_%d" % half)
-            nc.vector.tensor_tensor(
-                out=h4_sum[:],
-                in0=h4_acc[half][:].rearrange("c t b -> c b t"),
-                in1=b4_sb[:, half, :].unsqueeze(1).to_broadcast([P, BATCH, PACK]),
-                op=ADD,
-            )
+            h4_tiles = sbuf.tile([P, PACK, BATCH], BF16, name="h4_tiles_%d" % half)
+            for t in range(PACK):
+                nc.scalar.activation(
+                    out=h4_tiles[:, t, :],
+                    in_=h4_acc[half][:, t, :],
+                    func=mybir.ActivationFunctionType.Relu,
+                    bias=b4_sb[:, half, t : t + 1],
+                    scale=1.0,
+                )
+            return h4_tiles
+
+        def regroup_h4(half, h4_tiles):
             h4_grouped = sbuf.tile([P, BATCH, PACK], BF16, align_bytes=64, name="h4_grouped_%d" % half)
-            nc.vector.tensor_scalar_max(out=h4_grouped[:], in0=h4_sum[:], scalar1=0.0)
+            nc.vector.tensor_copy(out=h4_grouped[:], in_=h4_tiles[:].rearrange("c t b -> c b t"))
             return h4_grouped
 
-        def second_layer(half, h4_grouped):
+        def quantise_h4(half, h4_grouped):
             nc.vector.quantize_mx(
                 out=h4_codes[:, half, :].bitcast(FP8X4),
                 scales=h4_scales[:, half, :],
                 in_=h4_grouped[:].rearrange("c b t -> c (b t)"),
             )
+
+        def second_layer(half):
             nc.tensor.matmul_mx(
                 out=m_acc[:],
                 lhsT=h4_codes[:, half, :].bitcast(FP8X4),
@@ -146,6 +154,11 @@ def tile_additivecoupling_pa_s_kernel(tc, x, h3, W4, b4, W5, b5, out):
         regroup_w4(0, 0)
         nc.scalar.copy(out=res[:], in_=x_sb[:])
         quantise_w4(0, 0, VECTOR_TILES)
+        b5_all = psum.tile([BATCH, HALF], F32)
+        nc.tensor.matmul(b5_all[:], lhsT=ones[:], rhs=b5_rows[:], start=True, stop=True)
+        shift = sbuf.tile([BATCH, HALF], F32)
+        x_even = x_sb[:].rearrange("b (j two) -> b j two", two=2)[:, :, 0]
+        nc.vector.tensor_tensor(out=shift[:], in0=b5_all[:], in1=x_even, op=ADD)
 
         regroup_w4(0, 1)
         h3_words = h3_sb[:].bitcast(F32).rearrange("b (g p u) -> b g u p", g=PASSES, u=2)
@@ -154,22 +167,19 @@ def tile_additivecoupling_pa_s_kernel(tc, x, h3, W4, b4, W5, b5, out):
             for u in range(2):
                 nc.tensor.transpose(h3_t[:, g, u, :], h3_words[:, g, u, :], ident[:])
         h3_grouped = sbuf.tile([P, PASSES * BATCH * PACK], BF16, align_bytes=64)
-        nc.scalar.copy(
+        quantise_w4(0, 0, SCALAR_TILES)
+        quantise_w4(0, 1, VECTOR_TILES)
+        nc.vector.tensor_copy(
             out=h3_grouped[:].bitcast(F32).rearrange("p (g b u) -> p g b u", g=PASSES, u=2),
             in_=h3_t[:].rearrange("p g u b -> p g b u"),
         )
-        b5_all = psum.tile([BATCH, HALF], F32)
-        nc.tensor.matmul(b5_all[:], lhsT=ones[:], rhs=b5_rows[:], start=True, stop=True)
-        quantise_w4(0, 0, SCALAR_TILES)
-        quantise_w4(0, 1, VECTOR_TILES)
-        nc.vector.tensor_tensor(out=res_even, in0=b5_all[:], in1=res_even, op=ADD)
+
+        regroup_w4(1, 0)
         nc.vector.quantize_mx(
             out=h3_codes[:].rearrange("p g b -> p (g b)").bitcast(FP8X4),
             scales=h3_scales[:].rearrange("p g b -> p (g b)"),
             in_=h3_grouped[:],
         )
-
-        regroup_w4(1, 0)
         quantise_w4(0, 1, SCALAR_TILES)
         first_layer(0)
         quantise_w4(1, 0, VECTOR_TILES)
@@ -182,15 +192,16 @@ def tile_additivecoupling_pa_s_kernel(tc, x, h3, W4, b4, W5, b5, out):
         quantise_w4(1, 1, SCALAR_TILES)
         first_layer(1)
 
-        h4_grouped_0 = bias_relu(0)
         nc.vector.quantize_mx(
             out=w5_codes[:].rearrange("c g j -> c (g j)").bitcast(FP8X4),
             scales=w5_scales[:].rearrange("c g j -> c (g j)"),
             in_=w5_grouped[:].rearrange("c g j t -> c (g j t)"),
         )
-        second_layer(0, h4_grouped_0)
-        h4_grouped_1 = bias_relu(1)
-        second_layer(1, h4_grouped_1)
+        for half in range(PASSES):
+            h4_tiles = bias_relu(half)
+            h4_grouped = regroup_h4(half, h4_tiles)
+            quantise_h4(half, h4_grouped)
+            second_layer(half)
 
-        nc.vector.tensor_tensor(out=res_even, in0=m_acc[:], in1=res_even, op=ADD)
+        nc.vector.tensor_tensor(out=res_even, in0=m_acc[:], in1=shift[:], op=ADD)
         nc.sync.dma_start(out=out, in_=res[:])

@@ -18,6 +18,8 @@ MID = 1024
 HALF = 128
 PASSES = MID // K_PASS
 
+PARTS = {(0, 0): 2, (0, 1): 1, (1, 0): 1, (1, 1): 1}
+
 VECTOR_TILES = slice(0, 2)
 SCALAR_TILES = slice(2, 4)
 
@@ -41,18 +43,23 @@ def tile_additivecoupling_pa_s_kernel(tc, x, h3, W4, b4, W5, b5, out):
         w4_raw = {}
         for half in range(PASSES):
             for g in range(PASSES):
-                w4_raw[(half, g)] = sbuf.tile([P, PACK, K_PASS], BF16, name="w4_raw_%d%d" % (half, g))
+                for part in range(PARTS[(half, g)]):
+                    w4_raw[(half, g, part)] = sbuf.tile(
+                        [P, PACK, K_PASS // PARTS[(half, g)]], BF16, name="w4_raw_%d%d%d" % (half, g, part)
+                    )
         w4_rows = W4.rearrange("(g p j) n -> p g j n", g=PASSES, j=PACK)
         h3_sb = sbuf.tile([BATCH, MID], BF16)
         w5_raw = sbuf.tile([P, PASSES, PACK, HALF], BF16)
         x_sb = sbuf.tile([BATCH, 2 * HALF], BF16)
         b4_sb = sbuf.tile([P, PASSES, PACK], BF16)
 
-        def load_w4(half, g):
-            cols = slice(half * K_PASS, (half + 1) * K_PASS)
-            nc.sync.dma_start(out=w4_raw[(half, g)][:], in_=w4_rows[:, g, :, cols])
+        def load_w4(half, g, part=0):
+            width = K_PASS // PARTS[(half, g)]
+            cols = slice(half * K_PASS + part * width, half * K_PASS + (part + 1) * width)
+            nc.sync.dma_start(out=w4_raw[(half, g, part)][:], in_=w4_rows[:, g, :, cols])
 
-        load_w4(0, 0)
+        load_w4(0, 0, 0)
+        load_w4(0, 0, 1)
         nc.sync.dma_start(out=x_sb[:], in_=x)
         nc.sync.dma_start(out=b5_rows[0:1, :], in_=b5.rearrange("(o j) -> o j", o=1))
         nc.sync.dma_start(out=b4_sb[:], in_=b4.rearrange("(g c t) -> c g t", g=PASSES, t=PACK))
@@ -77,13 +84,17 @@ def tile_additivecoupling_pa_s_kernel(tc, x, h3, W4, b4, W5, b5, out):
         h4_codes = sbuf.tile([P, PASSES, BATCH], U32, align_bytes=64)
         h4_scales = sbuf.tile([P, PASSES, BATCH], U8, align_bytes=64)
         h4_acc = {}
-        for half in range(PASSES):
-            h4_acc[half] = psum.tile([P, PACK, BATCH], F32, name="h4_acc_%d" % half)
+        h4_bank_0 = psum.tile([P, PACK, BATCH], F32)
+        for t in range(PACK):
+            h4_acc[(0, t)] = h4_bank_0[:, t, :]
+            h4_bank_1 = psum.tile([P, BATCH], F32, name="h4_bank_1%d" % t)
+            h4_acc[(1, t)] = h4_bank_1[:]
         m_acc = psum.tile([BATCH, HALF], F32)
 
-        def regroup_w4(half, g):
-            dst = w4_grouped[(half, g)][:]
-            src = w4_raw[(half, g)][:].rearrange("p j (c t) -> p t c j", t=PACK)
+        def regroup_w4(half, g, part=0):
+            places = P // PARTS[(half, g)]
+            dst = w4_grouped[(half, g)][:, :, part * places : (part + 1) * places, :]
+            src = w4_raw[(half, g, part)][:].rearrange("p j (c t) -> p t c j", t=PACK)
             nc.vector.tensor_copy(
                 out=dst[:, VECTOR_TILES].rearrange("p t c j -> p c j t"),
                 in_=src[:, VECTOR_TILES].rearrange("p t c j -> p c j t"),
@@ -100,25 +111,23 @@ def tile_additivecoupling_pa_s_kernel(tc, x, h3, W4, b4, W5, b5, out):
                 in_=w4_grouped[(half, g)][:, tiles].rearrange("p t c j -> p (t c j)"),
             )
 
-        def first_layer(half):
-            for t in range(PACK):
-                for g in range(PASSES):
-                    nc.tensor.matmul_mx(
-                        out=h4_acc[half][:, t, :],
-                        lhsT=w4_codes[:, g, half, t, :].bitcast(FP8X4),
-                        lhsT_scale=w4_scales[:, g, half, t, :],
-                        rhs=h3_codes[:, g, :].bitcast(FP8X4),
-                        rhs_scale=h3_scales[:, g, :],
-                        start=(g == 0),
-                        stop=(g == PASSES - 1),
-                    )
+        def first_layer_pass(half, t, g):
+            nc.tensor.matmul_mx(
+                out=h4_acc[(half, t)],
+                lhsT=w4_codes[:, g, half, t, :].bitcast(FP8X4),
+                lhsT_scale=w4_scales[:, g, half, t, :],
+                rhs=h3_codes[:, g, :].bitcast(FP8X4),
+                rhs_scale=h3_scales[:, g, :],
+                start=(g == 0),
+                stop=(g == PASSES - 1),
+            )
 
         def bias_relu(half):
             h4_tiles = sbuf.tile([P, PACK, BATCH], BF16, name="h4_tiles_%d" % half)
             for t in range(PACK):
                 nc.scalar.activation(
                     out=h4_tiles[:, t, :],
-                    in_=h4_acc[half][:, t, :],
+                    in_=h4_acc[(half, t)],
                     func=mybir.ActivationFunctionType.Relu,
                     bias=b4_sb[:, half, t : t + 1],
                     scale=1.0,
@@ -151,7 +160,8 @@ def tile_additivecoupling_pa_s_kernel(tc, x, h3, W4, b4, W5, b5, out):
         res = sbuf.tile([BATCH, 2 * HALF], F32)
         res_even = res[:].rearrange("b (j two) -> b j two", two=2)[:, :, 0]
 
-        regroup_w4(0, 0)
+        regroup_w4(0, 0, 0)
+        regroup_w4(0, 0, 1)
         nc.scalar.copy(out=res[:], in_=x_sb[:])
         quantise_w4(0, 0, VECTOR_TILES)
         b5_all = psum.tile([BATCH, HALF], F32)
@@ -181,16 +191,23 @@ def tile_additivecoupling_pa_s_kernel(tc, x, h3, W4, b4, W5, b5, out):
             in_=h3_grouped[:],
         )
         quantise_w4(0, 1, SCALAR_TILES)
-        first_layer(0)
+        for t in range(PACK):
+            for g in range(PASSES):
+                first_layer_pass(0, t, g)
         quantise_w4(1, 0, VECTOR_TILES)
 
         regroup_w4(1, 1)
         w5_grouped = sbuf.tile([P, PASSES, HALF, PACK], BF16, align_bytes=64)
         nc.scalar.copy(out=w5_grouped[:], in_=w5_raw[:].rearrange("c g t j -> c g j t"))
         quantise_w4(1, 0, SCALAR_TILES)
+        for t in range(PACK):
+            first_layer_pass(1, t, 0)
         quantise_w4(1, 1, VECTOR_TILES)
+        first_layer_pass(1, 0, 1)
+        first_layer_pass(1, 1, 1)
         quantise_w4(1, 1, SCALAR_TILES)
-        first_layer(1)
+        first_layer_pass(1, 2, 1)
+        first_layer_pass(1, 3, 1)
 
         nc.vector.quantize_mx(
             out=w5_codes[:].rearrange("c g j -> c (g j)").bitcast(FP8X4),

@@ -197,8 +197,6 @@ def tile_additivecoupling_pa_s_kernel(tc, x, h3, W4, b4, W5, b5, out):
         quantise_w4(1, 0, VECTOR_TILES)
 
         regroup_w4(1, 1)
-        w5_grouped = sbuf.tile([P, PASSES, HALF, PACK], BF16, align_bytes=64)
-        nc.scalar.copy(out=w5_grouped[:], in_=w5_raw[:].rearrange("c g t j -> c g j t"))
         quantise_w4(1, 0, SCALAR_TILES)
         for t in range(PACK):
             first_layer_pass(1, t, 0)
@@ -209,16 +207,21 @@ def tile_additivecoupling_pa_s_kernel(tc, x, h3, W4, b4, W5, b5, out):
         first_layer_pass(1, 2, 1)
         first_layer_pass(1, 3, 1)
 
+        w5_grouped = sbuf.tile([P, PASSES, HALF, PACK], BF16, align_bytes=64)
+        nc.vector.tensor_copy(out=w5_grouped[:], in_=w5_raw[:].rearrange("c g t j -> c g j t"))
+        h4_tiles_0 = bias_relu(0)
+        h4_grouped_0 = regroup_h4(0, h4_tiles_0)
         nc.vector.quantize_mx(
             out=w5_codes[:].rearrange("c g j -> c (g j)").bitcast(FP8X4),
             scales=w5_scales[:].rearrange("c g j -> c (g j)"),
             in_=w5_grouped[:].rearrange("c g j t -> c (g j t)"),
         )
-        for half in range(PASSES):
-            h4_tiles = bias_relu(half)
-            h4_grouped = regroup_h4(half, h4_tiles)
-            quantise_h4(half, h4_grouped)
-            second_layer(half)
+        quantise_h4(0, h4_grouped_0)
+        second_layer(0)
+        h4_tiles_1 = bias_relu(1)
+        h4_grouped_1 = regroup_h4(1, h4_tiles_1)
+        quantise_h4(1, h4_grouped_1)
+        second_layer(1)
 
         nc.vector.tensor_tensor(out=res_even, in0=m_acc[:], in1=shift[:], op=ADD)
         nc.sync.dma_start(out=out, in_=res[:])

@@ -18,7 +18,7 @@ MID = 1024
 HALF = 128
 PASSES = MID // K_PASS
 
-PARTS = {(0, 0): 2, (0, 1): 1, (1, 0): 1, (1, 1): 1}
+PARTS = {(0, 0): 1, (0, 1): 1, (1, 0): 1, (1, 1): 1}
 
 VECTOR_TILES = slice(0, 2)
 SCALAR_TILES = slice(2, 4)
@@ -58,8 +58,7 @@ def tile_additivecoupling_pa_s_kernel(tc, x, h3, W4, b4, W5, b5, out):
             cols = slice(half * K_PASS + part * width, half * K_PASS + (part + 1) * width)
             nc.sync.dma_start(out=w4_raw[(half, g, part)][:], in_=w4_rows[:, g, :, cols])
 
-        load_w4(0, 0, 0)
-        load_w4(0, 0, 1)
+        load_w4(0, 0)
         nc.sync.dma_start(out=x_sb[:], in_=x)
         nc.sync.dma_start(out=b5_rows[0:1, :], in_=b5.rearrange("(o j) -> o j", o=1))
         nc.sync.dma_start(out=b4_sb[:], in_=b4.rearrange("(g c t) -> c g t", g=PASSES, t=PACK))
@@ -160,8 +159,7 @@ def tile_additivecoupling_pa_s_kernel(tc, x, h3, W4, b4, W5, b5, out):
         res = sbuf.tile([BATCH, 2 * HALF], F32)
         res_even = res[:].rearrange("b (j two) -> b j two", two=2)[:, :, 0]
 
-        regroup_w4(0, 0, 0)
-        regroup_w4(0, 0, 1)
+        regroup_w4(0, 0)
         nc.scalar.copy(out=res[:], in_=x_sb[:])
         quantise_w4(0, 0, VECTOR_TILES)
         b5_all = psum.tile([BATCH, HALF], F32)
@@ -216,10 +214,10 @@ def tile_additivecoupling_pa_s_kernel(tc, x, h3, W4, b4, W5, b5, out):
             scales=w5_scales[:].rearrange("c g j -> c (g j)"),
             in_=w5_grouped[:].rearrange("c g j t -> c (g j t)"),
         )
-        quantise_h4(0, h4_grouped_0)
-        second_layer(0)
         h4_tiles_1 = bias_relu(1)
         h4_grouped_1 = regroup_h4(1, h4_tiles_1)
+        quantise_h4(0, h4_grouped_0)
+        second_layer(0)
         quantise_h4(1, h4_grouped_1)
         second_layer(1)
 

@@ -35,6 +35,8 @@ def tile_additivecoupling_pa_s_kernel(tc, x, h3, W4, b4, W5, b5, out):
 
         ident = sbuf.tile([P, P], F32)
         make_identity(nc, ident[:])
+        ident_bf = sbuf.tile([P, P], BF16)
+        make_identity(nc, ident_bf[:])
         ones = sbuf.tile([P, BATCH], BF16)
         nc.vector.memset(ones[:], 1.0)
         b5_rows = sbuf.tile([P, HALF], BF16)
@@ -59,14 +61,14 @@ def tile_additivecoupling_pa_s_kernel(tc, x, h3, W4, b4, W5, b5, out):
             nc.sync.dma_start(out=w4_raw[(half, g, part)][:], in_=w4_rows[:, g, :, cols])
 
         load_w4(0, 0)
-        nc.sync.dma_start(out=x_sb[:], in_=x)
-        nc.sync.dma_start(out=b5_rows[0:1, :], in_=b5.rearrange("(o j) -> o j", o=1))
-        nc.sync.dma_start(out=b4_sb[:], in_=b4.rearrange("(g c t) -> c g t", g=PASSES, t=PACK))
         load_w4(0, 1)
         nc.sync.dma_start(out=h3_sb[:], in_=h3)
         load_w4(1, 0)
         load_w4(1, 1)
+        nc.sync.dma_start(out=b4_sb[:], in_=b4.rearrange("(g c t) -> c g t", g=PASSES, t=PACK))
         nc.sync.dma_start(out=w5_raw[:], in_=W5.rearrange("(g c t) j -> c g t j", g=PASSES, t=PACK))
+        nc.sync.dma_start(out=b5_rows[0:1, :], in_=b5.rearrange("(o j) -> o j", o=1))
+        nc.sync.dma_start(out=x_sb[:], in_=x)
 
         w4_grouped = {}
         for half in range(PASSES):
@@ -160,13 +162,7 @@ def tile_additivecoupling_pa_s_kernel(tc, x, h3, W4, b4, W5, b5, out):
         res_even = res[:].rearrange("b (j two) -> b j two", two=2)[:, :, 0]
 
         regroup_w4(0, 0)
-        nc.scalar.copy(out=res[:], in_=x_sb[:])
         quantise_w4(0, 0, VECTOR_TILES)
-        b5_all = psum.tile([BATCH, HALF], F32)
-        nc.tensor.matmul(b5_all[:], lhsT=ones[:], rhs=b5_rows[:], start=True, stop=True)
-        shift = sbuf.tile([BATCH, HALF], F32)
-        x_even = x_sb[:].rearrange("b (j two) -> b j two", two=2)[:, :, 0]
-        nc.vector.tensor_tensor(out=shift[:], in0=b5_all[:], in1=x_even, op=ADD)
 
         regroup_w4(0, 1)
         h3_words = h3_sb[:].bitcast(F32).rearrange("b (g p u) -> b g u p", g=PASSES, u=2)
@@ -177,7 +173,7 @@ def tile_additivecoupling_pa_s_kernel(tc, x, h3, W4, b4, W5, b5, out):
         h3_grouped = sbuf.tile([P, PASSES * BATCH * PACK], BF16, align_bytes=64)
         quantise_w4(0, 0, SCALAR_TILES)
         quantise_w4(0, 1, VECTOR_TILES)
-        nc.vector.tensor_copy(
+        nc.scalar.copy(
             out=h3_grouped[:].bitcast(F32).rearrange("p (g b u) -> p g b u", g=PASSES, u=2),
             in_=h3_t[:].rearrange("p g u b -> p g b u"),
         )
@@ -215,6 +211,13 @@ def tile_additivecoupling_pa_s_kernel(tc, x, h3, W4, b4, W5, b5, out):
             in_=w5_grouped[:].rearrange("c g j t -> c (g j t)"),
         )
         h4_tiles_1 = bias_relu(1)
+        shift_acc = psum.tile([BATCH, HALF], F32)
+        x_even = x_sb[:].rearrange("b (j two) -> b j two", two=2)[:, :, 0]
+        nc.tensor.matmul(shift_acc[:], lhsT=ones[:], rhs=b5_rows[:], start=True, stop=False)
+        nc.tensor.matmul(shift_acc[:], lhsT=ident_bf[:], rhs=x_even, start=False, stop=True)
+        nc.scalar.copy(out=res[:], in_=x_sb[:])
+        shift = sbuf.tile([BATCH, HALF], F32)
+        nc.scalar.copy(out=shift[:], in_=shift_acc[:])
         h4_grouped_1 = regroup_h4(1, h4_tiles_1)
         quantise_h4(0, h4_grouped_0)
         second_layer(0)

@@ -22,6 +22,7 @@ PARTS = {(0, 0): 1, (0, 1): 1, (1, 0): 1, (1, 1): 1}
 
 VECTOR_TILES = slice(0, 2)
 SCALAR_TILES = slice(2, 4)
+RUN = 4
 
 FLOPS = 2 * BATCH * MID * MID + 2 * BATCH * MID * HALF
 
@@ -53,7 +54,9 @@ def tile_additivecoupling_pa_s_kernel(tc, x, h3, W4, b4, W5, b5, out):
         h3_sb = sbuf.tile([BATCH, MID], BF16)
         w5_raw = sbuf.tile([P, PASSES, PACK, HALF], BF16)
         x_sb = sbuf.tile([BATCH, 2 * HALF], BF16)
-        b4_sb = sbuf.tile([P, PASSES, PACK], BF16)
+        b4_rows = sbuf.tile([P, P], BF16)
+        nc.vector.memset(b4_rows[:], 0.0)
+        b4_sb = sbuf.tile([P, PASSES * PACK], BF16)
 
         def load_w4(half, g, part=0):
             width = K_PASS // PARTS[(half, g)]
@@ -63,10 +66,10 @@ def tile_additivecoupling_pa_s_kernel(tc, x, h3, W4, b4, W5, b5, out):
         load_w4(0, 0)
         load_w4(0, 1)
         nc.sync.dma_start(out=h3_sb[:], in_=h3)
+        nc.sync.dma_start(out=b4_rows[0 : PASSES * PACK, :], in_=b4.rearrange("(t c) -> t c", c=P))
         load_w4(1, 0)
         load_w4(1, 1)
-        nc.sync.dma_start(out=b4_sb[:], in_=b4.rearrange("(g c t) -> c g t", g=PASSES, t=PACK))
-        nc.sync.dma_start(out=w5_raw[:], in_=W5.rearrange("(g c t) j -> c g t j", g=PASSES, t=PACK))
+        nc.sync.dma_start(out=w5_raw[:], in_=W5.rearrange("(g t c) j -> c g t j", g=PASSES, t=PACK))
         nc.sync.dma_start(out=b5_rows[0:1, :], in_=b5.rearrange("(o j) -> o j", o=1))
         nc.sync.dma_start(out=x_sb[:], in_=x)
 
@@ -93,17 +96,11 @@ def tile_additivecoupling_pa_s_kernel(tc, x, h3, W4, b4, W5, b5, out):
         m_acc = psum.tile([BATCH, HALF], F32)
 
         def regroup_w4(half, g, part=0):
-            places = P // PARTS[(half, g)]
-            dst = w4_grouped[(half, g)][:, :, part * places : (part + 1) * places, :]
-            src = w4_raw[(half, g, part)][:].rearrange("p j (c t) -> p t c j", t=PACK)
-            nc.vector.tensor_copy(
-                out=dst[:, VECTOR_TILES].rearrange("p t c j -> p c j t"),
-                in_=src[:, VECTOR_TILES].rearrange("p t c j -> p c j t"),
-            )
-            nc.scalar.copy(
-                out=dst[:, SCALAR_TILES].rearrange("p t c j -> p c j t"),
-                in_=src[:, SCALAR_TILES].rearrange("p t c j -> p c j t"),
-            )
+            dst = w4_grouped[(half, g)][:].rearrange("p t (c i) j -> p (t c) j i", i=RUN)
+            src = w4_raw[(half, g, part)][:].rearrange("p j (c i) -> p c j i", i=RUN)
+            mid = 2 * P // RUN
+            nc.vector.tensor_copy(out=dst[:, :mid], in_=src[:, :mid])
+            nc.scalar.copy(out=dst[:, mid:], in_=src[:, mid:])
 
         def quantise_w4(half, g, tiles):
             nc.vector.quantize_mx(
@@ -130,14 +127,17 @@ def tile_additivecoupling_pa_s_kernel(tc, x, h3, W4, b4, W5, b5, out):
                     out=h4_tiles[:, t, :],
                     in_=h4_acc[(half, t)],
                     func=mybir.ActivationFunctionType.Relu,
-                    bias=b4_sb[:, half, t : t + 1],
+                    bias=b4_sb[:, half * PACK + t : half * PACK + t + 1],
                     scale=1.0,
                 )
             return h4_tiles
 
         def regroup_h4(half, h4_tiles):
             h4_grouped = sbuf.tile([P, BATCH, PACK], BF16, align_bytes=64, name="h4_grouped_%d" % half)
-            nc.vector.tensor_copy(out=h4_grouped[:], in_=h4_tiles[:].rearrange("c t b -> c b t"))
+            nc.vector.tensor_copy(
+                out=h4_grouped[:].rearrange("c (b i) t -> c b t i", i=RUN),
+                in_=h4_tiles[:].rearrange("c t (b i) -> c b t i", i=RUN),
+            )
             return h4_grouped
 
         def quantise_h4(half, h4_grouped):
@@ -170,6 +170,8 @@ def tile_additivecoupling_pa_s_kernel(tc, x, h3, W4, b4, W5, b5, out):
         for g in range(PASSES):
             for u in range(2):
                 nc.tensor.transpose(h3_t[:, g, u, :], h3_words[:, g, u, :], ident[:])
+        b4_t = psum.tile([P, P], BF16, tag="b4_then_shift")
+        nc.tensor.transpose(b4_t[:], b4_rows[:], ident_bf[:])
         h3_grouped = sbuf.tile([P, PASSES * BATCH * PACK], BF16, align_bytes=64)
         quantise_w4(0, 0, SCALAR_TILES)
         quantise_w4(0, 1, VECTOR_TILES)
@@ -178,6 +180,7 @@ def tile_additivecoupling_pa_s_kernel(tc, x, h3, W4, b4, W5, b5, out):
             in_=h3_t[:].rearrange("p g u b -> p g b u"),
         )
 
+        nc.scalar.copy(out=b4_sb[:], in_=b4_t[:, 0 : PASSES * PACK])
         regroup_w4(1, 0)
         nc.vector.quantize_mx(
             out=h3_codes[:].rearrange("p g b -> p (g b)").bitcast(FP8X4),
@@ -202,7 +205,11 @@ def tile_additivecoupling_pa_s_kernel(tc, x, h3, W4, b4, W5, b5, out):
         first_layer_pass(1, 3, 1)
 
         w5_grouped = sbuf.tile([P, PASSES, HALF, PACK], BF16, align_bytes=64)
-        nc.vector.tensor_copy(out=w5_grouped[:], in_=w5_raw[:].rearrange("c g t j -> c g j t"))
+        for g in range(PASSES):
+            nc.vector.tensor_copy(
+                out=w5_grouped[:, g].rearrange("c (j i) t -> c j t i", i=RUN),
+                in_=w5_raw[:, g].rearrange("c t (j i) -> c j t i", i=RUN),
+            )
         h4_tiles_0 = bias_relu(0)
         h4_grouped_0 = regroup_h4(0, h4_tiles_0)
         nc.vector.quantize_mx(
@@ -211,7 +218,7 @@ def tile_additivecoupling_pa_s_kernel(tc, x, h3, W4, b4, W5, b5, out):
             in_=w5_grouped[:].rearrange("c g j t -> c (g j t)"),
         )
         h4_tiles_1 = bias_relu(1)
-        shift_acc = psum.tile([BATCH, HALF], F32)
+        shift_acc = psum.tile([BATCH, HALF], F32, tag="b4_then_shift")
         x_even = x_sb[:].rearrange("b (j two) -> b j two", two=2)[:, :, 0]
         nc.tensor.matmul(shift_acc[:], lhsT=ones[:], rhs=b5_rows[:], start=True, stop=False)
         nc.tensor.matmul(shift_acc[:], lhsT=ident_bf[:], rhs=x_even, start=False, stop=True)

@@ -17,12 +17,8 @@ BATCH = 128
 MID = 1024
 HALF = 128
 PASSES = MID // K_PASS
-
-PARTS = {(0, 0): 1, (0, 1): 1, (1, 0): 1, (1, 1): 1}
-
-VECTOR_TILES = slice(0, 2)
-SCALAR_TILES = slice(2, 4)
 RUN = 4
+VECTOR_COLUMNS = 256
 
 FLOPS = 2 * BATCH * MID * MID + 2 * BATCH * MID * HALF
 
@@ -42,114 +38,180 @@ def tile_additivecoupling_pa_s_kernel(tc, x, h3, W4, b4, W5, b5, out):
         nc.vector.memset(ones[:], 1.0)
         b5_rows = sbuf.tile([P, HALF], BF16)
         nc.vector.memset(b5_rows[:], 0.0)
+        b4_rows = sbuf.tile([P, P], BF16)
+        nc.vector.memset(b4_rows[:], 0.0)
 
+        w4_rows = W4.rearrange("(g p j) n -> p g j n", g=PASSES, j=PACK)
         w4_raw = {}
         for half in range(PASSES):
             for g in range(PASSES):
-                for part in range(PARTS[(half, g)]):
-                    w4_raw[(half, g, part)] = sbuf.tile(
-                        [P, PACK, K_PASS // PARTS[(half, g)]], BF16, name="w4_raw_%d%d%d" % (half, g, part)
-                    )
-        w4_rows = W4.rearrange("(g p j) n -> p g j n", g=PASSES, j=PACK)
+                w4_raw[(half, g)] = sbuf.tile([P, PACK, K_PASS], BF16, name="w4_raw_%d%d" % (half, g))
         h3_sb = sbuf.tile([BATCH, MID], BF16)
-        w5_raw = sbuf.tile([P, PASSES, PACK, HALF], BF16)
+        w5_raw = sbuf.tile([P, PACK, PASSES, HALF], BF16)
         x_sb = sbuf.tile([BATCH, 2 * HALF], BF16)
-        b4_rows = sbuf.tile([P, P], BF16)
-        nc.vector.memset(b4_rows[:], 0.0)
         b4_sb = sbuf.tile([P, PASSES * PACK], BF16)
 
-        def load_w4(half, g, part=0):
-            width = K_PASS // PARTS[(half, g)]
-            cols = slice(half * K_PASS + part * width, half * K_PASS + (part + 1) * width)
-            nc.sync.dma_start(out=w4_raw[(half, g, part)][:], in_=w4_rows[:, g, :, cols])
+        def load_w4(half, g):
+            cols = slice(half * K_PASS, (half + 1) * K_PASS)
+            nc.sync.dma_start(out=w4_raw[(half, g)][:], in_=w4_rows[:, g, :, cols])
+
+        def load_h3():
+            nc.sync.dma_start(out=h3_sb[:], in_=h3)
+
+        def load_b4():
+            nc.sync.dma_start(out=b4_rows[0 : PASSES * PACK, :], in_=b4.rearrange("(t c) -> t c", c=P))
+
+        def load_w5():
+            w5_rows = W5.rearrange("(g t c) j -> g c t j", g=PASSES, t=PACK)
+            for g in range(PASSES):
+                nc.sync.dma_start(out=w5_raw[:, :, g, :], in_=w5_rows[g])
+
+        def load_b5():
+            nc.sync.dma_start(out=b5_rows[0:1, :], in_=b5.rearrange("(o j) -> o j", o=1))
+
+        def load_x():
+            nc.sync.dma_start(out=x_sb[:], in_=x)
 
         load_w4(0, 0)
+        load_b4()
+        load_h3()
         load_w4(0, 1)
-        nc.sync.dma_start(out=h3_sb[:], in_=h3)
-        nc.sync.dma_start(out=b4_rows[0 : PASSES * PACK, :], in_=b4.rearrange("(t c) -> t c", c=P))
         load_w4(1, 0)
         load_w4(1, 1)
-        nc.sync.dma_start(out=w5_raw[:], in_=W5.rearrange("(g t c) j -> c g t j", g=PASSES, t=PACK))
-        nc.sync.dma_start(out=b5_rows[0:1, :], in_=b5.rearrange("(o j) -> o j", o=1))
-        nc.sync.dma_start(out=x_sb[:], in_=x)
+        load_w5()
+        load_b5()
+        load_x()
 
         w4_grouped = {}
         for half in range(PASSES):
             for g in range(PASSES):
                 w4_grouped[(half, g)] = sbuf.tile(
-                    [P, PACK, P, PACK], BF16, align_bytes=64, name="w4_grouped_%d%d" % (half, g)
+                    [P, K_PASS, PACK], BF16, align_bytes=64, name="w4_grouped_%d%d" % (half, g)
                 )
-        w4_codes = sbuf.tile([P, PASSES, PASSES, PACK, P], U32, align_bytes=64)
-        w4_scales = sbuf.tile([P, PASSES, PASSES, PACK, P], U8, align_bytes=64)
+        w4_codes = sbuf.tile([P, PASSES, PASSES, K_PASS], U32, align_bytes=64)
+        w4_scales = sbuf.tile([P, PASSES, PASSES, K_PASS], U8, align_bytes=64)
         h3_codes = sbuf.tile([P, PASSES, BATCH], U32, align_bytes=64)
         h3_scales = sbuf.tile([P, PASSES, BATCH], U8, align_bytes=64)
         w5_codes = sbuf.tile([P, PASSES, HALF], U32, align_bytes=64)
         w5_scales = sbuf.tile([P, PASSES, HALF], U8, align_bytes=64)
         h4_codes = sbuf.tile([P, PASSES, BATCH], U32, align_bytes=64)
         h4_scales = sbuf.tile([P, PASSES, BATCH], U8, align_bytes=64)
+        h3_grouped = sbuf.tile([P, PASSES * BATCH * PACK], BF16, align_bytes=64)
+        w5_grouped = sbuf.tile([P, PASSES, HALF, PACK], BF16, align_bytes=64)
+        h4_tiles = {}
+        h4_grouped = {}
+        for half in range(PASSES):
+            h4_tiles[half] = sbuf.tile([P, PACK, BATCH], BF16, name="h4_tiles_%d" % half)
+            h4_grouped[half] = sbuf.tile([P, BATCH, PACK], BF16, align_bytes=64, name="h4_grouped_%d" % half)
+        res = sbuf.tile([BATCH, 2 * HALF], F32)
+        shift = sbuf.tile([BATCH, 2, HALF], F32)
+        nc.gpsimd.memset(shift[:, 1, :], 0.0)
         h4_acc = {}
         h4_bank_0 = psum.tile([P, PACK, BATCH], F32)
         for t in range(PACK):
             h4_acc[(0, t)] = h4_bank_0[:, t, :]
             h4_bank_1 = psum.tile([P, BATCH], F32, name="h4_bank_1%d" % t)
             h4_acc[(1, t)] = h4_bank_1[:]
-        m_acc = psum.tile([BATCH, HALF], F32)
+        m_and_odd = psum.tile([BATCH, 2, HALF], F32)
+        m_acc = m_and_odd[:, 0, :]
+        h3_t = psum.tile([P, PASSES, 2, BATCH], F32)
+        b4_t = psum.tile([P, P], BF16, tag="b4_then_shift")
 
-        def regroup_w4(half, g, part=0):
-            dst = w4_grouped[(half, g)][:].rearrange("p t (c i) j -> p (t c) j i", i=RUN)
-            src = w4_raw[(half, g, part)][:].rearrange("p j (c i) -> p c j i", i=RUN)
-            mid = 2 * P // RUN
-            nc.vector.tensor_copy(out=dst[:, :mid], in_=src[:, :mid])
-            nc.scalar.copy(out=dst[:, mid:], in_=src[:, mid:])
-
-        def quantise_w4(half, g, tiles):
-            nc.vector.quantize_mx(
-                out=w4_codes[:, g, half, tiles].rearrange("p t c -> p (t c)").bitcast(FP8X4),
-                scales=w4_scales[:, g, half, tiles].rearrange("p t c -> p (t c)"),
-                in_=w4_grouped[(half, g)][:, tiles].rearrange("p t c j -> p (t c j)"),
+        def regroup(copy, half, g, first, last):
+            copy(
+                out=w4_grouped[(half, g)][:, first:last, :].rearrange("p (c i) j -> p c j i", i=RUN),
+                in_=w4_raw[(half, g)][:, :, first:last].rearrange("p j (c i) -> p c j i", i=RUN),
             )
 
+        def regroup_vector(half, g, cols=VECTOR_COLUMNS):
+            regroup(nc.vector.tensor_copy, half, g, 0, cols)
+
+        def regroup_scalar(half, g, cols=VECTOR_COLUMNS):
+            regroup(nc.scalar.copy, half, g, cols, K_PASS)
+
+        def quantise_w4(half, g, first, last):
+            cols = slice(first * P, last * P)
+            nc.vector.quantize_mx(
+                out=w4_codes[:, g, half, cols].bitcast(FP8X4),
+                scales=w4_scales[:, g, half, cols],
+                in_=w4_grouped[(half, g)][:, cols].rearrange("p c j -> p (c j)"),
+            )
+
+        def transpose_h3():
+            h3_words = h3_sb[:].bitcast(F32).rearrange("b (g p u) -> b g u p", g=PASSES, u=2)
+            for g in range(PASSES):
+                for u in range(2):
+                    nc.tensor.transpose(h3_t[:, g, u, :], h3_words[:, g, u, :], ident[:])
+
+        def copy_h3():
+            nc.scalar.copy(
+                out=h3_grouped[:].bitcast(F32).rearrange("p (g b u) -> p g b u", g=PASSES, u=2),
+                in_=h3_t[:].rearrange("p g u b -> p g b u"),
+            )
+
+        def quantise_h3():
+            nc.vector.quantize_mx(
+                out=h3_codes[:].rearrange("p g b -> p (g b)").bitcast(FP8X4),
+                scales=h3_scales[:].rearrange("p g b -> p (g b)"),
+                in_=h3_grouped[:],
+            )
+
+        def transpose_b4():
+            nc.tensor.transpose(b4_t[:], b4_rows[:], ident_bf[:])
+
+        def copy_b4():
+            nc.scalar.copy(out=b4_sb[:], in_=b4_t[:, 0 : PASSES * PACK])
+
         def first_layer_pass(half, t, g):
+            cols = slice(t * P, (t + 1) * P)
             nc.tensor.matmul_mx(
                 out=h4_acc[(half, t)],
-                lhsT=w4_codes[:, g, half, t, :].bitcast(FP8X4),
-                lhsT_scale=w4_scales[:, g, half, t, :],
+                lhsT=w4_codes[:, g, half, cols].bitcast(FP8X4),
+                lhsT_scale=w4_scales[:, g, half, cols],
                 rhs=h3_codes[:, g, :].bitcast(FP8X4),
                 rhs_scale=h3_scales[:, g, :],
                 start=(g == 0),
                 stop=(g == PASSES - 1),
             )
 
-        def bias_relu(half):
-            h4_tiles = sbuf.tile([P, PACK, BATCH], BF16, name="h4_tiles_%d" % half)
-            for t in range(PACK):
-                nc.scalar.activation(
-                    out=h4_tiles[:, t, :],
-                    in_=h4_acc[(half, t)],
-                    func=mybir.ActivationFunctionType.Relu,
-                    bias=b4_sb[:, half * PACK + t : half * PACK + t + 1],
-                    scale=1.0,
-                )
-            return h4_tiles
-
-        def regroup_h4(half, h4_tiles):
-            h4_grouped = sbuf.tile([P, BATCH, PACK], BF16, align_bytes=64, name="h4_grouped_%d" % half)
-            nc.vector.tensor_copy(
-                out=h4_grouped[:].rearrange("c (b i) t -> c b t i", i=RUN),
-                in_=h4_tiles[:].rearrange("c t (b i) -> c b t i", i=RUN),
+        def bias_relu(half, t):
+            nc.scalar.activation(
+                out=h4_tiles[half][:, t, :],
+                in_=h4_acc[(half, t)],
+                func=mybir.ActivationFunctionType.Relu,
+                bias=b4_sb[:, half * PACK + t : half * PACK + t + 1],
+                scale=1.0,
             )
-            return h4_grouped
 
-        def quantise_h4(half, h4_grouped):
+        def regroup_h4(half):
+            nc.vector.tensor_copy(
+                out=h4_grouped[half][:].rearrange("c (b i) t -> c b t i", i=RUN),
+                in_=h4_tiles[half][:].rearrange("c t (b i) -> c b t i", i=RUN),
+            )
+
+        def quantise_h4(half):
             nc.vector.quantize_mx(
                 out=h4_codes[:, half, :].bitcast(FP8X4),
                 scales=h4_scales[:, half, :],
-                in_=h4_grouped[:].rearrange("c b t -> c (b t)"),
+                in_=h4_grouped[half][:].rearrange("c b t -> c (b t)"),
+            )
+
+        def regroup_w5():
+            nc.vector.tensor_copy(
+                out=w5_grouped[:].rearrange("c g (j i) t -> c (g j) t i", i=RUN),
+                in_=w5_raw[:].rearrange("c t g (j i) -> c (g j) t i", i=RUN),
+            )
+
+        def quantise_w5():
+            nc.vector.quantize_mx(
+                out=w5_codes[:].rearrange("c g j -> c (g j)").bitcast(FP8X4),
+                scales=w5_scales[:].rearrange("c g j -> c (g j)"),
+                in_=w5_grouped[:].rearrange("c g j t -> c (g j t)"),
             )
 
         def second_layer(half):
             nc.tensor.matmul_mx(
-                out=m_acc[:],
+                out=m_acc,
                 lhsT=h4_codes[:, half, :].bitcast(FP8X4),
                 lhsT_scale=h4_scales[:, half, :],
                 rhs=w5_codes[:, half, :].bitcast(FP8X4),
@@ -158,78 +220,66 @@ def tile_additivecoupling_pa_s_kernel(tc, x, h3, W4, b4, W5, b5, out):
                 stop=(half == PASSES - 1),
             )
 
-        res = sbuf.tile([BATCH, 2 * HALF], F32)
-        res_even = res[:].rearrange("b (j two) -> b j two", two=2)[:, :, 0]
+        def shift_matmuls():
+            shift_acc = psum.tile([BATCH, HALF], F32, tag="b4_then_shift")
+            x_even = x_sb[:].rearrange("b (j two) -> b j two", two=2)[:, :, 0]
+            x_odd = x_sb[:].rearrange("b (j two) -> b j two", two=2)[:, :, 1]
+            nc.tensor.matmul(m_and_odd[:, 1, :], lhsT=ident_bf[:], rhs=x_odd, start=True, stop=True)
+            nc.tensor.matmul(shift_acc[:], lhsT=ones[:], rhs=b5_rows[:], start=True, stop=False)
+            nc.tensor.matmul(shift_acc[:], lhsT=ident_bf[:], rhs=x_even, start=False, stop=True)
+            return shift_acc
 
-        regroup_w4(0, 0)
-        quantise_w4(0, 0, VECTOR_TILES)
+        def finish():
+            nc.vector.tensor_tensor(
+                out=res[:].rearrange("b (j two) -> b j two", two=2),
+                in0=m_and_odd[:].rearrange("b two j -> b j two"),
+                in1=shift[:].rearrange("b two j -> b j two"),
+                op=ADD,
+            )
+            nc.sync.dma_start(out=out, in_=res[:])
 
-        regroup_w4(0, 1)
-        h3_words = h3_sb[:].bitcast(F32).rearrange("b (g p u) -> b g u p", g=PASSES, u=2)
-        h3_t = psum.tile([P, PASSES, 2, BATCH], F32)
-        for g in range(PASSES):
-            for u in range(2):
-                nc.tensor.transpose(h3_t[:, g, u, :], h3_words[:, g, u, :], ident[:])
-        b4_t = psum.tile([P, P], BF16, tag="b4_then_shift")
-        nc.tensor.transpose(b4_t[:], b4_rows[:], ident_bf[:])
-        h3_grouped = sbuf.tile([P, PASSES * BATCH * PACK], BF16, align_bytes=64)
-        quantise_w4(0, 0, SCALAR_TILES)
-        quantise_w4(0, 1, VECTOR_TILES)
-        nc.scalar.copy(
-            out=h3_grouped[:].bitcast(F32).rearrange("p (g b u) -> p g b u", g=PASSES, u=2),
-            in_=h3_t[:].rearrange("p g u b -> p g b u"),
-        )
-
-        nc.scalar.copy(out=b4_sb[:], in_=b4_t[:, 0 : PASSES * PACK])
-        regroup_w4(1, 0)
-        nc.vector.quantize_mx(
-            out=h3_codes[:].rearrange("p g b -> p (g b)").bitcast(FP8X4),
-            scales=h3_scales[:].rearrange("p g b -> p (g b)"),
-            in_=h3_grouped[:],
-        )
-        quantise_w4(0, 1, SCALAR_TILES)
+        regroup_vector(0, 0)
+        regroup_scalar(0, 0)
+        transpose_b4()
+        transpose_h3()
+        quantise_w4(0, 0, 0, 2)
+        quantise_w4(0, 0, 2, 4)
+        copy_b4()
+        copy_h3()
+        regroup_vector(0, 1)
+        regroup_scalar(0, 1)
+        quantise_h3()
+        quantise_w4(0, 1, 0, 2)
+        regroup_vector(1, 0)
+        regroup_scalar(1, 0)
+        quantise_w4(0, 1, 2, 4)
         for t in range(PACK):
             for g in range(PASSES):
                 first_layer_pass(0, t, g)
-        quantise_w4(1, 0, VECTOR_TILES)
-
-        regroup_w4(1, 1)
-        quantise_w4(1, 0, SCALAR_TILES)
+        quantise_w4(1, 0, 0, 2)
+        regroup_vector(1, 1)
+        regroup_scalar(1, 1)
+        quantise_w4(1, 0, 2, 4)
         for t in range(PACK):
             first_layer_pass(1, t, 0)
-        quantise_w4(1, 1, VECTOR_TILES)
+        quantise_w4(1, 1, 0, 2)
         first_layer_pass(1, 0, 1)
         first_layer_pass(1, 1, 1)
-        quantise_w4(1, 1, SCALAR_TILES)
+        quantise_w4(1, 1, 2, 4)
         first_layer_pass(1, 2, 1)
         first_layer_pass(1, 3, 1)
-
-        w5_grouped = sbuf.tile([P, PASSES, HALF, PACK], BF16, align_bytes=64)
-        for g in range(PASSES):
-            nc.vector.tensor_copy(
-                out=w5_grouped[:, g].rearrange("c (j i) t -> c j t i", i=RUN),
-                in_=w5_raw[:, g].rearrange("c t (j i) -> c j t i", i=RUN),
-            )
-        h4_tiles_0 = bias_relu(0)
-        h4_grouped_0 = regroup_h4(0, h4_tiles_0)
-        nc.vector.quantize_mx(
-            out=w5_codes[:].rearrange("c g j -> c (g j)").bitcast(FP8X4),
-            scales=w5_scales[:].rearrange("c g j -> c (g j)"),
-            in_=w5_grouped[:].rearrange("c g j t -> c (g j t)"),
-        )
-        h4_tiles_1 = bias_relu(1)
-        shift_acc = psum.tile([BATCH, HALF], F32, tag="b4_then_shift")
-        x_even = x_sb[:].rearrange("b (j two) -> b j two", two=2)[:, :, 0]
-        nc.tensor.matmul(shift_acc[:], lhsT=ones[:], rhs=b5_rows[:], start=True, stop=False)
-        nc.tensor.matmul(shift_acc[:], lhsT=ident_bf[:], rhs=x_even, start=False, stop=True)
-        nc.scalar.copy(out=res[:], in_=x_sb[:])
-        shift = sbuf.tile([BATCH, HALF], F32)
-        nc.scalar.copy(out=shift[:], in_=shift_acc[:])
-        h4_grouped_1 = regroup_h4(1, h4_tiles_1)
-        quantise_h4(0, h4_grouped_0)
+        regroup_w5()
+        for t in range(PACK):
+            bias_relu(0, t)
+        regroup_h4(0)
+        quantise_w5()
+        for t in range(PACK):
+            bias_relu(1, t)
+        shift_acc = shift_matmuls()
+        nc.scalar.copy(out=shift[:, 0, :], in_=shift_acc[:])
+        regroup_h4(1)
+        quantise_h4(0)
         second_layer(0)
-        quantise_h4(1, h4_grouped_1)
+        quantise_h4(1)
         second_layer(1)
-
-        nc.vector.tensor_tensor(out=res_even, in0=m_acc[:], in1=shift[:], op=ADD)
-        nc.sync.dma_start(out=out, in_=res[:])
+        finish()

@@ -33,13 +33,13 @@ def tile_additivecoupling_pa_s_kernel(tc, x, h3, W4, b4, W5, b5, out):
         ident = sbuf.tile([P, P], F32)
         make_identity(nc, ident[:])
         ident_bf = sbuf.tile([P, P], BF16)
-        make_identity(nc, ident_bf[:])
         ones = sbuf.tile([P, BATCH], BF16)
         nc.vector.memset(ones[:], 1.0)
         b5_rows = sbuf.tile([P, HALF], BF16)
         nc.vector.memset(b5_rows[:], 0.0)
         b4_rows = sbuf.tile([P, P], BF16)
         nc.vector.memset(b4_rows[:], 0.0)
+        nc.vector.tensor_copy(out=ident_bf[:], in_=ident[:])
 
         w4_rows = W4.rearrange("(g p j) n -> p g j n", g=PASSES, j=PACK)
         w4_raw = {}
@@ -78,9 +78,9 @@ def tile_additivecoupling_pa_s_kernel(tc, x, h3, W4, b4, W5, b5, out):
         load_w4(0, 1)
         load_w4(1, 0)
         load_w4(1, 1)
-        load_w5()
-        load_b5()
         load_x()
+        load_b5()
+        load_w5()
 
         w4_grouped = {}
         for half in range(PASSES):

from contextlib import ExitStack

import concourse.mybir as mybir
from concourse.masks import make_identity

BF16 = mybir.dt.bfloat16
F32 = mybir.dt.float32
U32 = mybir.dt.uint32
U8 = mybir.dt.uint8
FP8X4 = mybir.dt.float8_e4m3fn_x4
ADD = mybir.AluOpType.add

P = 128
PACK = 4
K_PASS = P * PACK
BATCH = 128
MID = 1024
HALF = 128
PASSES = MID // K_PASS
RUN = 4
VECTOR_COLUMNS = 256

FLOPS = 2 * BATCH * MID * MID + 2 * BATCH * MID * HALF


def tile_additivecoupling_pa_s_kernel(tc, x, h3, W4, b4, W5, b5, out):
    nc = tc.nc
    with ExitStack() as stack:
        sbuf = stack.enter_context(tc.tile_pool(name="sbuf", bufs=1))
        psum = stack.enter_context(tc.psum_pool(name="psum", bufs=1))
        stack.enter_context(tc.manual_schedule())

        ident = sbuf.tile([P, P], F32)
        make_identity(nc, ident[:])
        ident_bf = sbuf.tile([P, P], BF16)
        ones = sbuf.tile([P, BATCH], BF16)
        nc.vector.memset(ones[:], 1.0)
        b5_rows = sbuf.tile([P, HALF], BF16)
        nc.vector.memset(b5_rows[:], 0.0)
        b4_rows = sbuf.tile([P, P], BF16)
        nc.vector.memset(b4_rows[:], 0.0)
        nc.vector.tensor_copy(out=ident_bf[:], in_=ident[:])

        w4_rows = W4.rearrange("(g p j) n -> p g j n", g=PASSES, j=PACK)
        w4_raw = {}
        for half in range(PASSES):
            for g in range(PASSES):
                w4_raw[(half, g)] = sbuf.tile([P, PACK, K_PASS], BF16, name="w4_raw_%d%d" % (half, g))
        h3_sb = sbuf.tile([BATCH, MID], BF16)
        w5_raw = sbuf.tile([P, PACK, PASSES, HALF], BF16)
        x_sb = sbuf.tile([BATCH, 2 * HALF], BF16)
        b4_sb = sbuf.tile([P, PASSES * PACK], BF16)

        def load_w4(half, g):
            cols = slice(half * K_PASS, (half + 1) * K_PASS)
            nc.sync.dma_start(out=w4_raw[(half, g)][:], in_=w4_rows[:, g, :, cols])

        def load_h3():
            nc.sync.dma_start(out=h3_sb[:], in_=h3)

        def load_b4():
            nc.sync.dma_start(out=b4_rows[0 : PASSES * PACK, :], in_=b4.rearrange("(t c) -> t c", c=P))

        def load_w5():
            w5_rows = W5.rearrange("(g t c) j -> g c t j", g=PASSES, t=PACK)
            for g in range(PASSES):
                nc.sync.dma_start(out=w5_raw[:, :, g, :], in_=w5_rows[g])

        def load_b5():
            nc.sync.dma_start(out=b5_rows[0:1, :], in_=b5.rearrange("(o j) -> o j", o=1))

        def load_x():
            nc.sync.dma_start(out=x_sb[:], in_=x)

        load_w4(0, 0)
        load_b4()
        load_h3()
        load_w4(0, 1)
        load_w4(1, 0)
        load_w4(1, 1)
        load_x()
        load_b5()
        load_w5()

        w4_grouped = {}
        for half in range(PASSES):
            for g in range(PASSES):
                w4_grouped[(half, g)] = sbuf.tile(
                    [P, K_PASS, PACK], BF16, align_bytes=64, name="w4_grouped_%d%d" % (half, g)
                )
        w4_codes = sbuf.tile([P, PASSES, PASSES, K_PASS], U32, align_bytes=64)
        w4_scales = sbuf.tile([P, PASSES, PASSES, K_PASS], U8, align_bytes=64)
        h3_codes = sbuf.tile([P, PASSES, BATCH], U32, align_bytes=64)
        h3_scales = sbuf.tile([P, PASSES, BATCH], U8, align_bytes=64)
        w5_codes = sbuf.tile([P, PASSES, HALF], U32, align_bytes=64)
        w5_scales = sbuf.tile([P, PASSES, HALF], U8, align_bytes=64)
        h4_codes = sbuf.tile([P, PASSES, BATCH], U32, align_bytes=64)
        h4_scales = sbuf.tile([P, PASSES, BATCH], U8, align_bytes=64)
        h3_grouped = sbuf.tile([P, PASSES * BATCH * PACK], BF16, align_bytes=64)
        w5_grouped = sbuf.tile([P, PASSES, HALF, PACK], BF16, align_bytes=64)
        h4_tiles = {}
        h4_grouped = {}
        for half in range(PASSES):
            h4_tiles[half] = sbuf.tile([P, PACK, BATCH], BF16, name="h4_tiles_%d" % half)
            h4_grouped[half] = sbuf.tile([P, BATCH, PACK], BF16, align_bytes=64, name="h4_grouped_%d" % half)
        res = sbuf.tile([BATCH, 2 * HALF], F32)
        shift = sbuf.tile([BATCH, 2, HALF], F32)
        nc.gpsimd.memset(shift[:, 1, :], 0.0)
        h4_acc = {}
        h4_bank_0 = psum.tile([P, PACK, BATCH], F32)
        for t in range(PACK):
            h4_acc[(0, t)] = h4_bank_0[:, t, :]
            h4_bank_1 = psum.tile([P, BATCH], F32, name="h4_bank_1%d" % t)
            h4_acc[(1, t)] = h4_bank_1[:]
        m_and_odd = psum.tile([BATCH, 2, HALF], F32)
        m_acc = m_and_odd[:, 0, :]
        h3_t = psum.tile([P, PASSES, 2, BATCH], F32)
        b4_t = psum.tile([P, P], BF16, tag="b4_then_shift")

        def regroup(copy, half, g, first, last):
            copy(
                out=w4_grouped[(half, g)][:, first:last, :].rearrange("p (c i) j -> p c j i", i=RUN),
                in_=w4_raw[(half, g)][:, :, first:last].rearrange("p j (c i) -> p c j i", i=RUN),
            )

        def regroup_vector(half, g, cols=VECTOR_COLUMNS):
            regroup(nc.vector.tensor_copy, half, g, 0, cols)

        def regroup_scalar(half, g, cols=VECTOR_COLUMNS):
            regroup(nc.scalar.copy, half, g, cols, K_PASS)

        def quantise_w4(half, g, first, last):
            cols = slice(first * P, last * P)
            nc.vector.quantize_mx(
                out=w4_codes[:, g, half, cols].bitcast(FP8X4),
                scales=w4_scales[:, g, half, cols],
                in_=w4_grouped[(half, g)][:, cols].rearrange("p c j -> p (c j)"),
            )

        def transpose_h3():
            h3_words = h3_sb[:].bitcast(F32).rearrange("b (g p u) -> b g u p", g=PASSES, u=2)
            for g in range(PASSES):
                for u in range(2):
                    nc.tensor.transpose(h3_t[:, g, u, :], h3_words[:, g, u, :], ident[:])

        def copy_h3():
            nc.scalar.copy(
                out=h3_grouped[:].bitcast(F32).rearrange("p (g b u) -> p g b u", g=PASSES, u=2),
                in_=h3_t[:].rearrange("p g u b -> p g b u"),
            )

        def quantise_h3():
            nc.vector.quantize_mx(
                out=h3_codes[:].rearrange("p g b -> p (g b)").bitcast(FP8X4),
                scales=h3_scales[:].rearrange("p g b -> p (g b)"),
                in_=h3_grouped[:],
            )

        def transpose_b4():
            nc.tensor.transpose(b4_t[:], b4_rows[:], ident_bf[:])

        def copy_b4():
            nc.scalar.copy(out=b4_sb[:], in_=b4_t[:, 0 : PASSES * PACK])

        def first_layer_pass(half, t, g):
            cols = slice(t * P, (t + 1) * P)
            nc.tensor.matmul_mx(
                out=h4_acc[(half, t)],
                lhsT=w4_codes[:, g, half, cols].bitcast(FP8X4),
                lhsT_scale=w4_scales[:, g, half, cols],
                rhs=h3_codes[:, g, :].bitcast(FP8X4),
                rhs_scale=h3_scales[:, g, :],
                start=(g == 0),
                stop=(g == PASSES - 1),
            )

        def bias_relu(half, t):
            nc.scalar.activation(
                out=h4_tiles[half][:, t, :],
                in_=h4_acc[(half, t)],
                func=mybir.ActivationFunctionType.Relu,
                bias=b4_sb[:, half * PACK + t : half * PACK + t + 1],
                scale=1.0,
            )

        def regroup_h4(half):
            nc.vector.tensor_copy(
                out=h4_grouped[half][:].rearrange("c (b i) t -> c b t i", i=RUN),
                in_=h4_tiles[half][:].rearrange("c t (b i) -> c b t i", i=RUN),
            )

        def quantise_h4(half):
            nc.vector.quantize_mx(
                out=h4_codes[:, half, :].bitcast(FP8X4),
                scales=h4_scales[:, half, :],
                in_=h4_grouped[half][:].rearrange("c b t -> c (b t)"),
            )

        def regroup_w5():
            nc.vector.tensor_copy(
                out=w5_grouped[:].rearrange("c g (j i) t -> c (g j) t i", i=RUN),
                in_=w5_raw[:].rearrange("c t g (j i) -> c (g j) t i", i=RUN),
            )

        def quantise_w5():
            nc.vector.quantize_mx(
                out=w5_codes[:].rearrange("c g j -> c (g j)").bitcast(FP8X4),
                scales=w5_scales[:].rearrange("c g j -> c (g j)"),
                in_=w5_grouped[:].rearrange("c g j t -> c (g j t)"),
            )

        def second_layer(half):
            nc.tensor.matmul_mx(
                out=m_acc,
                lhsT=h4_codes[:, half, :].bitcast(FP8X4),
                lhsT_scale=h4_scales[:, half, :],
                rhs=w5_codes[:, half, :].bitcast(FP8X4),
                rhs_scale=w5_scales[:, half, :],
                start=(half == 0),
                stop=(half == PASSES - 1),
            )

        def shift_matmuls():
            shift_acc = psum.tile([BATCH, HALF], F32, tag="b4_then_shift")
            x_even = x_sb[:].rearrange("b (j two) -> b j two", two=2)[:, :, 0]
            x_odd = x_sb[:].rearrange("b (j two) -> b j two", two=2)[:, :, 1]
            nc.tensor.matmul(m_and_odd[:, 1, :], lhsT=ident_bf[:], rhs=x_odd, start=True, stop=True)
            nc.tensor.matmul(shift_acc[:], lhsT=ones[:], rhs=b5_rows[:], start=True, stop=False)
            nc.tensor.matmul(shift_acc[:], lhsT=ident_bf[:], rhs=x_even, start=False, stop=True)
            return shift_acc

        def finish():
            nc.vector.tensor_tensor(
                out=res[:].rearrange("b (j two) -> b j two", two=2),
                in0=m_and_odd[:].rearrange("b two j -> b j two"),
                in1=shift[:].rearrange("b two j -> b j two"),
                op=ADD,
            )
            nc.sync.dma_start(out=out, in_=res[:])

        regroup_vector(0, 0)
        regroup_scalar(0, 0)
        transpose_b4()
        transpose_h3()
        quantise_w4(0, 0, 0, 2)
        quantise_w4(0, 0, 2, 4)
        copy_b4()
        copy_h3()
        regroup_vector(0, 1)
        regroup_scalar(0, 1)
        quantise_h3()
        quantise_w4(0, 1, 0, 2)
        regroup_vector(1, 0)
        regroup_scalar(1, 0)
        quantise_w4(0, 1, 2, 4)
        for t in range(PACK):
            for g in range(PASSES):
                first_layer_pass(0, t, g)
        quantise_w4(1, 0, 0, 2)
        regroup_vector(1, 1)
        regroup_scalar(1, 1)
        quantise_w4(1, 0, 2, 4)
        for t in range(PACK):
            first_layer_pass(1, t, 0)
        quantise_w4(1, 1, 0, 2)
        first_layer_pass(1, 0, 1)
        first_layer_pass(1, 1, 1)
        quantise_w4(1, 1, 2, 4)
        first_layer_pass(1, 2, 1)
        first_layer_pass(1, 3, 1)
        regroup_w5()
        for t in range(PACK):
            bias_relu(0, t)
        regroup_h4(0)
        quantise_w5()
        for t in range(PACK):
            bias_relu(1, t)
        shift_acc = shift_matmuls()
        nc.scalar.copy(out=shift[:, 0, :], in_=shift_acc[:])
        regroup_h4(1)
        quantise_h4(0)
        second_layer(0)
        quantise_h4(1)
        second_layer(1)
        finish()
